import numpy as np
import ml_dtypes


def mxq(x, axis, fmt="e4m3"):
    dtype, down = {"e4m3": (ml_dtypes.float8_e4m3fn, 7), "e5m2": (ml_dtypes.float8_e5m2, 14)}[fmt]
    v = np.moveaxis(np.asarray(x, np.float32).astype(ml_dtypes.bfloat16).astype(np.float64), axis, -1)
    blocks = v.reshape(v.shape[:-1] + (-1, 32))
    amax = np.abs(blocks).max(-1, keepdims=True)
    byte = np.maximum(np.where(amax > 0, np.frexp(amax)[1] - 1 + 127, 0) - down, 1)
    scale = np.exp2(byte - 127.0)
    codes = (blocks / scale).astype(np.float32).astype(dtype).astype(np.float64)
    return np.moveaxis((codes * scale).reshape(v.shape), -1, axis)


WIDE = False


def mx_kscale(k):
    if not WIDE:
        return np.ones(k)
    levels = np.array([10, -10, 5, -5, 0])
    a = np.random.permutation(np.resize(levels, k // 512 * 4)).reshape(k // 512, 4)
    idx = np.arange(k)
    return np.exp2(a[idx // 512, idx % 128 // 32])


BF16 = ml_dtypes.bfloat16


def bf(x):
    return np.asarray(x, np.float32).astype(BF16)


def f64(x):
    return np.asarray(x).astype(np.float64)


E2M1 = np.array([0.0, 0.5, 1.0, 1.5, 2.0, 3.0, 4.0, 6.0, -0.0, -0.5, -1.0, -1.5, -2.0, -3.0, -4.0, -6.0])


def pack_weight(w, fmt):
    k, n = w.shape
    w = f64(bf(w)).reshape(k // 32, 32, n)
    amax = np.abs(w).max(1)
    if fmt == "e4m3":
        byte = np.frexp(amax)[1] - 1 + 127 - 7
    else:
        mant, ex = np.frexp(amax / 6.0)
        byte = np.where(mant > 0.5, ex, ex - 1) + 127
    byte = np.clip(np.where(amax > 0, byte, 1), 1, 254)
    scaled = (w * np.exp2(127.0 - byte)[:, None, :]).reshape(k, n).astype(np.float32)
    by_word = np.ascontiguousarray(scaled.reshape(k // 512, 128, 4, n).transpose(0, 1, 3, 2))
    if fmt == "e4m3":
        words = by_word.astype(ml_dtypes.float8_e4m3fn).view(np.uint8)
    else:
        c = by_word.astype(ml_dtypes.float4_e2m1fn).view(np.uint8) & 0xF
        words = c[..., 0::2] | (c[..., 1::2] << 4)
    return np.ascontiguousarray(words), np.ascontiguousarray(byte.astype(np.uint8).reshape(k // 512, 16, n))


def unpack_weight(words, scales, fmt):
    g, p, n, _ = words.shape
    if fmt == "e4m3":
        vals = np.ascontiguousarray(words).view(ml_dtypes.float8_e4m3fn).astype(np.float64)
    else:
        nib = np.empty((g, p, n, 4), np.uint8)
        nib[..., 0::2] = words & 0xF
        nib[..., 1::2] = words >> 4
        vals = E2M1[nib]
    vals = vals * np.repeat(np.exp2(scales.astype(np.float64) - 127.0), 8, axis=1)[..., None]
    return vals.transpose(0, 1, 3, 2).reshape(g * 512, n)


N, F, E, H, R = 128, 8192, 3072, 4, 8
EPS = 1e-6


def setup_inputs():
    s = mx_kscale(F)
    c = 4.0 / np.sqrt(E)
    B = np.random.standard_normal((R, E)) / np.sqrt(R)
    W = c * (0.8 * np.random.standard_normal((F, R)) @ B + 0.6 * np.random.standard_normal((F, E))) / np.sqrt(F)
    Z = c * (0.8 * np.random.standard_normal((H, N, R)) @ B + 0.6 * np.random.standard_normal((H, N, E)))
    W_words, W_scales = pack_weight(W / s[:, None], "e4m3")
    return {"X": bf(np.random.standard_normal((N, F)) * s), "W_words": W_words, "W_scales": W_scales, "Z": bf(Z),
            "beta": bf(1.5 + 0.5 * np.random.random(1))}


def reference(X, W_words, W_scales, Z, beta):
    Zf = f64(Z)
    X_emb = mxq(f64(X), 1, "e4m3") @ unpack_weight(W_words, W_scales, "e4m3")
    aff = mxq(Zf, 2, "e4m3") @ mxq(X_emb, 1, "e4m3").T
    X_norm = np.sqrt(np.sum(X_emb * X_emb, axis=-1))
    Z_norm = np.sqrt(np.sum(Zf * Zf, axis=-1))
    aff = aff / (X_norm[None, None, :] + EPS)
    aff = aff / (Z_norm[:, :, None] + EPS)
    aff = np.max(aff, axis=0)
    aff = (aff + aff.T) / 2.0
    aff = (aff + 1.0) / 2.0
    return np.power(aff, f64(beta))

@@ -1,0 +1,294 @@
+from contextlib import ExitStack
+
+import concourse.mybir as mybir
+from concourse.masks import make_identity
+
+BF16 = mybir.dt.bfloat16
+F32 = mybir.dt.float32
+I32 = mybir.dt.int32
+U32 = mybir.dt.uint32
+U8 = mybir.dt.uint8
+FP8X4 = mybir.dt.float8_e4m3fn_x4
+ACT = mybir.ActivationFunctionType
+ALU = mybir.AluOpType
+AX = mybir.AxisListType
+
+P = 128
+F_DIM = 8192
+E_DIM = 3072
+HEADS = 4
+K_PASS = 512
+G1 = F_DIM // K_PASS
+G2 = E_DIM // K_PASS
+EPS = 1e-6
+A_BANKS = 5
+A_COLS = A_BANKS * 512
+RING = 9
+B_GROUPS = ((0, 4), (4, 4), (8, 4), (12, 2), (14, 1), (15, 1))
+
+FLOPS = 2 * P * F_DIM * E_DIM + 2 * HEADS * P * P * E_DIM
+
+
+def tile_affnet_w_kernel(tc, X, W_words, W_scales, Z, beta, out):
+    nc = tc.nc
+    with ExitStack() as ctx:
+        keep = ctx.enter_context(tc.tile_pool(name="keep", bufs=1))
+        grp = ctx.enter_context(tc.tile_pool(name="grp", bufs=3))
+        ring = ctx.enter_context(tc.tile_pool(name="ring", bufs=RING))
+        xegp = ctx.enter_context(tc.tile_pool(name="xegp", bufs=2))
+        psum = ctx.enter_context(tc.psum_pool(name="psum", bufs=1))
+
+        def bank(i, label, shape=(P, 512), dtype=F32):
+            return psum.tile(list(shape), dtype, tag="bank%d" % i, name=label)
+
+        x_sb = [keep.tile([P, 4096], BF16, name="x%d" % i, tag="x%d" % i) for i in range(2)]
+        z_sb = [keep.tile([P, E_DIM], BF16, name="z%d" % h, tag="z%d" % h) for h in range(HEADS)]
+        planes = keep.tile([P, 4, E_DIM], U8, name="planes", tag="planes", align_bytes=64)
+        xcodes = keep.tile([P, G1 * P], U32, name="xcodes", tag="xcodes", align_bytes=64)
+        xplane = keep.tile([P, G1 * P], U8, name="xplane", tag="xplane", align_bytes=64)
+        zcodes = keep.tile([P, G2 * 512], U32, name="zcodes", tag="zcodes", align_bytes=64)
+        zplane = keep.tile([P, G2 * 512], U8, name="zplane", tag="zplane", align_bytes=64)
+        xecodes = keep.tile([P, G2 * P], U32, name="xecodes", tag="xecodes", align_bytes=64)
+        xeplane = keep.tile([P, G2 * P], U8, name="xeplane", tag="xeplane", align_bytes=64)
+        ident_f = keep.tile([P, P], F32, name="ident_f", tag="ident_f")
+        ident_b = keep.tile([P, P], BF16, name="ident_b", tag="ident_b")
+        beta_b = keep.tile([P, 1], BF16, name="beta_b", tag="beta_b")
+        beta_f = keep.tile([P, 1], F32, name="beta_f", tag="beta_f")
+        half = keep.tile([P, 1], F32, name="half", tag="half")
+        zjunk = keep.tile([P, E_DIM], BF16, name="zjunk", tag="zjunk")
+        xjunk = keep.tile([P, 512], BF16, name="xjunk", tag="xjunk")
+        zss = keep.tile([P, HEADS], F32, name="zss", tag="zss")
+        zn = keep.tile([P, HEADS], F32, name="zn", tag="zn")
+        zne = keep.tile([P, HEADS], F32, name="zne", tag="zne")
+        rz = keep.tile([P, HEADS], F32, name="rz", tag="rz")
+        rep = keep.tile([P, HEADS, P], F32, name="rep", tag="rep")
+        rz_all = keep.tile([P, HEADS * P], F32, name="rz_all", tag="rz_all")
+        xss = keep.tile([P, G2], F32, name="xss", tag="xss")
+        xss_a = keep.tile([P, 1], F32, name="xss_a", tag="xss_a")
+        xn = keep.tile([P, 1], F32, name="xn", tag="xn")
+        lnjunk = keep.tile([P, 1], F32, name="lnjunk", tag="lnjunk")
+        xne = keep.tile([P, 1], F32, name="xne", tag="xne")
+        rx = keep.tile([P, 1], F32, name="rx", tag="rx")
+        scaled = keep.tile([P, HEADS * P], F32, name="scaled", tag="scaled")
+        max2 = keep.tile([P, 2 * P], F32, name="max2", tag="max2")
+        cosT = keep.tile([P, P], F32, name="cosT", tag="cosT")
+        sym = keep.tile([P, P], F32, name="sym", tag="sym")
+        logv = keep.tile([P, P], F32, name="logv", tag="logv")
+        res = keep.tile([P, P], F32, name="res", tag="res")
+        xe = [keep.tile([P, 4, P], BF16, name="xe%d" % b, tag="xe%d" % b) for b in range(G2)]
+
+        for i in range(2):
+            nc.sync.dma_start(out=x_sb[i][:], in_=X[:, 4096 * i : 4096 * (i + 1)])
+        nc.scalar.dma_start(out=beta_b[:], in_=beta.partition_broadcast(P))
+        for s in range(4):
+            nc.vector.memset(planes[:, s, :].bitcast(I32), 0)
+        nc.vector.memset(half[:], 0.5)
+        make_identity(nc, ident_f[:])
+        make_identity(nc, ident_b[:])
+        for s in range(4):
+            for q in range(4):
+                nc.sync.dma_start(
+                    out=planes[32 * q : 32 * q + 16, s, :].bitcast(I32),
+                    in_=W_scales[4 * s : 4 * s + 4, 4 * q : 4 * q + 4, :].bitcast(I32),
+                )
+        for h in range(HEADS):
+            nc.sync.dma_start(out=z_sb[h][:], in_=Z[h])
+
+        w_loads = [("A", g, 1) for g in range(G1)] + [("B", g0, n) for (g0, n) in B_GROUPS]
+        w_tiles = {}
+
+        def load_w(i):
+            if i >= len(w_loads):
+                return
+            kind, g0, n = w_loads[i]
+            if kind == "A":
+                wt = ring.tile([P, A_COLS], I32, name="wa%d" % g0, tag="w", align_bytes=64)
+                src = W_words[g0].rearrange("p n t -> p (n t)")[:, 0 : 4 * A_COLS].bitcast(I32)
+            else:
+                wt = ring.tile([P, n, 512], I32, name="wb%d" % g0, tag="w", align_bytes=64)
+                src = (
+                    W_words[g0 : g0 + n]
+                    .rearrange("g p n t -> p g (n t)")[:, :, 4 * A_COLS : 4 * E_DIM]
+                    .bitcast(I32)
+                )
+            nc.sync.dma_start(out=wt[:], in_=src)
+            w_tiles[i] = wt
+
+        for i in range(RING):
+            load_w(i)
+
+        nc.vector.tensor_copy(out=beta_f[:], in_=beta_b[:])
+
+        def flip_words(words_of, dst, part, bank_i, label, engine):
+            bk = bank(bank_i, label)
+            for a in range(2):
+                for u in range(2):
+                    nc.tensor.transpose(
+                        bk[:, (2 * a + u) * P : (2 * a + u + 1) * P], words_of(a, u), ident_f[:]
+                    )
+            o = dst[:].bitcast(F32)[:, 512 * part : 512 * (part + 1)].rearrange(
+                "p (a n u) -> p a n u", a=2, u=2
+            )
+            i = bk[:].rearrange("p (a u n) -> p a n u", a=2, u=2)
+            if engine == "v":
+                nc.vector.tensor_copy(out=o, in_=i)
+            else:
+                nc.scalar.copy(out=o, in_=i)
+
+        def quant(src, codes, plane, lo, width):
+            nc.vector.quantize_mx(
+                out=codes[:, lo : lo + width].bitcast(FP8X4),
+                scales=plane[:, lo : lo + width],
+                in_=src,
+            )
+
+        def x_words(j, part):
+            def pick(a, u):
+                g = 4 * j + 2 * part + a
+                xw = x_sb[g // 8][:].bitcast(F32)
+                lo = 256 * (g % 8)
+                return xw[:, lo + u : lo + 256 : 2]
+
+            return pick
+
+        def z_words(c, part):
+            def pick(a, u):
+                zw = z_sb[2 * part + a][:].bitcast(F32)
+                return zw[:, 256 * c + u : 256 * (c + 1) : 2]
+
+            return pick
+
+        pending = None
+        for j in range(4):
+            xg = grp.tile([P, 2048], BF16, name="xg%d" % j, tag="grp", align_bytes=64)
+            flip_words(x_words(j, 0), xg, 0, 2 * j, "xt%da" % j, "v")
+            flip_words(x_words(j, 1), xg, 1, 2 * j + 1, "xt%db" % j, "s")
+            if pending is not None:
+                quant(pending[0][:], xcodes, xplane, 512 * pending[1], 512)
+            pending = (xg, j)
+        quant(pending[0][:], xcodes, xplane, 512 * pending[1], 512)
+
+        pending = None
+        for c in range(G2):
+            zg = grp.tile([P, 2048], BF16, name="zg%d" % c, tag="grp", align_bytes=64)
+            flip_words(z_words(c, 0), zg, 0, 5 + (2 * c) % 3, "zt%da" % c, "v")
+            flip_words(z_words(c, 1), zg, 1, 5 + (2 * c + 1) % 3, "zt%db" % c, "s")
+            if pending is not None:
+                quant(pending[0][:], zcodes, zplane, 512 * pending[1], 512)
+            pending = (zg, c)
+        quant(pending[0][:], zcodes, zplane, 512 * pending[1], 512)
+
+        for h in range(HEADS):
+            nc.scalar.activation(
+                out=zjunk[:], in_=z_sb[h][:], func=ACT.Square, accum_out=zss[:, h : h + 1]
+            )
+        nc.scalar.activation(out=zn[:], in_=zss[:], func=ACT.Sqrt)
+        nc.vector.tensor_scalar_add(out=zne[:], in0=zn[:], scalar1=EPS)
+        nc.vector.reciprocal(out=rz[:], in_=zne[:])
+        nc.vector.tensor_copy(out=rep[:], in_=rz[:].unsqueeze(2).to_broadcast([P, HEADS, P]))
+
+        def w_pass(acc, g, codes, col0):
+            k = 4 * (g % 4)
+            nc.tensor.matmul_mx(
+                out=acc[:],
+                lhsT=xcodes[:, P * g : P * (g + 1)].bitcast(FP8X4),
+                lhsT_scale=xplane[:, P * g : P * (g + 1)],
+                rhs=codes.bitcast(FP8X4),
+                rhs_scale=planes[k:P, g // 4, col0 : col0 + 512],
+                start=(g == 0),
+                stop=(g == G1 - 1),
+            )
+
+        acc = [bank(b, "acc%d" % b) for b in range(A_BANKS)]
+        for g in range(G1):
+            wt = w_tiles[g]
+            for b in range(A_BANKS):
+                w_pass(acc[b], g, wt[:, 512 * b : 512 * (b + 1)], 512 * b)
+            load_w(g + RING)
+            if g == 7:
+                rzb = bank(7, "rzb")
+                for h in range(HEADS):
+                    nc.tensor.transpose(rzb[:, P * h : P * (h + 1)], rep[:, h, :], ident_f[:])
+                nc.scalar.copy(out=rz_all[:], in_=rzb[:])
+
+        def evacuate(b, src):
+            nc.vector.tensor_copy(out=xe[b][:], in_=src[:].rearrange("p (q t) -> p t q", t=4))
+            nc.scalar.activation(
+                out=xjunk[:], in_=src[:], func=ACT.Square, accum_out=xss[:, b : b + 1]
+            )
+
+        def flip_xe(bs, bank_i, engine):
+            n = len(bs)
+            xt = bank(bank_i, "xet%d" % bs[0], (P, n, 4, P), BF16)
+            for i, b in enumerate(bs):
+                for t in range(4):
+                    nc.tensor.transpose(xt[:, i, t, :], xe[b][:, t, :], ident_b[:])
+            xeg = xegp.tile([P, n * 512], BF16, name="xeg%d" % bs[0], tag="xeg", align_bytes=64)
+            o = xeg[:].rearrange("p (i n t) -> p i n t", i=n, t=4)
+            src = xt[:].rearrange("p i t n -> p i n t")
+            if engine == "v":
+                nc.vector.tensor_copy(out=o, in_=src)
+            else:
+                nc.scalar.copy(out=o, in_=src)
+            quant(xeg[:], xecodes, xeplane, P * bs[0], P * n)
+
+        aff = bank(6, "aff")
+
+        def aff_pass(c):
+            nc.tensor.matmul_mx(
+                out=aff[:],
+                lhsT=xecodes[:, P * c : P * (c + 1)].bitcast(FP8X4),
+                lhsT_scale=xeplane[:, P * c : P * (c + 1)],
+                rhs=zcodes[:, 512 * c : 512 * (c + 1)].bitcast(FP8X4),
+                rhs_scale=zplane[:, 512 * c : 512 * (c + 1)],
+                start=(c == 0),
+                stop=(c == G2 - 1),
+            )
+
+        acc_b = bank(5, "accb")
+
+        def b_passes(i):
+            kind, g0, n = w_loads[i]
+            wt = w_tiles[i]
+            for gi in range(n):
+                w_pass(acc_b, g0 + gi, wt[:, gi, :], A_COLS)
+            load_w(i + RING)
+
+        for b in range(A_BANKS):
+            evacuate(b, acc[b])
+        nc.vector.tensor_reduce(out=xss_a[:], in_=xss[:, 0:A_BANKS], op=ALU.add, axis=AX.X)
+        flip_xe([0, 1], 7, "s")
+        b_passes(G1)
+        flip_xe([2, 3], 0, "s")
+        flip_xe([4], 1, "s")
+        aff_pass(0)
+        aff_pass(1)
+        b_passes(G1 + 1)
+        aff_pass(2)
+        aff_pass(3)
+        aff_pass(4)
+        for i in range(G1 + 2, len(w_loads)):
+            b_passes(i)
+
+        last = G2 - 1
+        evacuate(last, acc_b)
+        nc.scalar.activation(
+            out=xn[:], in_=xss[:, last : last + 1], func=ACT.Sqrt, bias=xss_a[:, 0:1]
+        )
+        nc.scalar.activation(out=lnjunk[:], in_=xn[:], func=ACT.Ln)
+        flip_xe([last], 2, "v")
+        nc.vector.tensor_scalar_add(out=xne[:], in0=xn[:], scalar1=EPS)
+        nc.vector.reciprocal(out=rx[:], in_=xne[:])
+        aff_pass(last)
+
+        nc.vector.scalar_tensor_tensor(
+            out=scaled[:], in0=aff[:], scalar=rx[:, 0:1], in1=rz_all[:], op0=ALU.mult, op1=ALU.mult
+        )
+        nc.vector.tensor_max(out=max2[:], in0=scaled[:, 0 : 2 * P], in1=scaled[:, 2 * P : 4 * P])
+        nc.vector.tensor_max(out=cosT[:], in0=max2[:, 0:P], in1=max2[:, P : 2 * P])
+        cos_b = bank(3, "cosb")
+        nc.tensor.transpose(cos_b[:, 0:P], cosT[:], ident_f[:])
+        nc.vector.tensor_add(out=sym[:], in0=cosT[:], in1=cos_b[:, 0:P])
+        nc.scalar.activation(out=logv[:], in_=sym[:], func=ACT.Ln, scale=0.25, bias=half[:, 0:1])
+        nc.scalar.activation(out=res[:], in_=logv[:], func=ACT.Exp, scale=beta_f[:, 0:1])
+        nc.sync.dma_start(out=out[:, :], in_=res[:])

@@ -84,13 +84,14 @@ def tile_affnet_w_kernel(tc, X, W_words, W_scales, Z, beta, out):
             nc.vector.memset(planes[:, s, :].bitcast(I32), 0)
         nc.vector.memset(half[:], 0.5)
         make_identity(nc, ident_f[:])
-        make_identity(nc, ident_b[:])
         for s in range(4):
             for q in range(4):
-                nc.sync.dma_start(
-                    out=planes[32 * q : 32 * q + 16, s, :].bitcast(I32),
-                    in_=W_scales[4 * s : 4 * s + 4, 4 * q : 4 * q + 4, :].bitcast(I32),
+                nc.gpsimd.dma_start(
+                    out=planes[32 * q : 32 * q + 16, s, :].bitcast(F32),
+                    in_=W_scales[4 * s : 4 * s + 4, 4 * q : 4 * q + 4, :].bitcast(F32),
                 )
+            if s == 0:
+                make_identity(nc, ident_b[:])
         for h in range(HEADS):
             nc.sync.dma_start(out=z_sb[h][:], in_=Z[h])
 

@@ -11,6 +11,7 @@ U8 = mybir.dt.uint8
 FP8X4 = mybir.dt.float8_e4m3fn_x4
 ACT = mybir.ActivationFunctionType
 ALU = mybir.AluOpType
+ENG = mybir.EngineType
 AX = mybir.AxisListType
 
 P = 128
@@ -159,35 +160,6 @@ def tile_affnet_w_kernel(tc, X, W_words, W_scales, Z, beta, out):
 
             return pick
 
-        pending = None
-        for j in range(4):
-            xg = grp.tile([P, 2048], BF16, name="xg%d" % j, tag="grp", align_bytes=64)
-            flip_words(x_words(j, 0), xg, 0, 2 * j, "xt%da" % j, "v")
-            flip_words(x_words(j, 1), xg, 1, 2 * j + 1, "xt%db" % j, "s")
-            if pending is not None:
-                quant(pending[0][:], xcodes, xplane, 512 * pending[1], 512)
-            pending = (xg, j)
-        quant(pending[0][:], xcodes, xplane, 512 * pending[1], 512)
-
-        pending = None
-        for c in range(G2):
-            zg = grp.tile([P, 2048], BF16, name="zg%d" % c, tag="grp", align_bytes=64)
-            flip_words(z_words(c, 0), zg, 0, 5 + (2 * c) % 3, "zt%da" % c, "v")
-            flip_words(z_words(c, 1), zg, 1, 5 + (2 * c + 1) % 3, "zt%db" % c, "s")
-            if pending is not None:
-                quant(pending[0][:], zcodes, zplane, 512 * pending[1], 512)
-            pending = (zg, c)
-        quant(pending[0][:], zcodes, zplane, 512 * pending[1], 512)
-
-        for h in range(HEADS):
-            nc.scalar.activation(
-                out=zjunk[:], in_=z_sb[h][:], func=ACT.Square, accum_out=zss[:, h : h + 1]
-            )
-        nc.scalar.activation(out=zn[:], in_=zss[:], func=ACT.Sqrt)
-        nc.vector.tensor_scalar_add(out=zne[:], in0=zn[:], scalar1=EPS)
-        nc.vector.reciprocal(out=rz[:], in_=zne[:])
-        nc.vector.tensor_copy(out=rep[:], in_=rz[:].unsqueeze(2).to_broadcast([P, HEADS, P]))
-
         def w_pass(acc, g, codes, col0):
             k = 4 * (g % 4)
             nc.tensor.matmul_mx(
@@ -200,17 +172,41 @@ def tile_affnet_w_kernel(tc, X, W_words, W_scales, Z, beta, out):
                 stop=(g == G1 - 1),
             )
 
-        acc = [bank(b, "acc%d" % b) for b in range(A_BANKS)]
-        for g in range(G1):
-            wt = w_tiles[g]
-            for b in range(A_BANKS):
-                w_pass(acc[b], g, wt[:, 512 * b : 512 * (b + 1)], 512 * b)
-            load_w(g + RING)
-            if g == 7:
-                rzb = bank(7, "rzb")
-                for h in range(HEADS):
-                    nc.tensor.transpose(rzb[:, P * h : P * (h + 1)], rep[:, h, :], ident_f[:])
-                nc.scalar.copy(out=rz_all[:], in_=rzb[:])
+        with tc.manual_schedule(engines={ENG.PE, ENG.DVE, ENG.Activation}):
+            jobs = [(x_words, j, xcodes, xplane) for j in range(4)]
+            jobs += [(z_words, c, zcodes, zplane) for c in range(G2)]
+            pending = None
+            for i, (words, j, codes, plane) in enumerate(jobs):
+                og = grp.tile([P, 2048], BF16, name="og%d" % i, tag="grp", align_bytes=64)
+                flip_words(words(j, 0), og, 0, (2 * i) % 8, "ot%da" % i, "v")
+                flip_words(words(j, 1), og, 1, (2 * i + 1) % 8, "ot%db" % i, "s")
+                if pending is not None:
+                    quant(*pending)
+                pending = (og[:], codes, plane, 512 * j, 512)
+            quant(*pending)
+
+            acc = [bank(b, "acc%d" % b) for b in range(A_BANKS)]
+            for g in range(G1):
+                wt = w_tiles[g]
+                for b in range(A_BANKS):
+                    w_pass(acc[b], g, wt[:, 512 * b : 512 * (b + 1)], 512 * b)
+                load_w(g + RING)
+                if g < HEADS:
+                    nc.scalar.activation(
+                        out=zjunk[:], in_=z_sb[g][:], func=ACT.Square, accum_out=zss[:, g : g + 1]
+                    )
+                if g == HEADS:
+                    nc.scalar.activation(out=zn[:], in_=zss[:], func=ACT.Sqrt)
+                    nc.vector.tensor_scalar_add(out=zne[:], in0=zn[:], scalar1=EPS)
+                    nc.vector.reciprocal(out=rz[:], in_=zne[:])
+                    nc.vector.tensor_copy(
+                        out=rep[:], in_=rz[:].unsqueeze(2).to_broadcast([P, HEADS, P])
+                    )
+                if g == 10:
+                    rzb = bank(7, "rzb")
+                    for h in range(HEADS):
+                        nc.tensor.transpose(rzb[:, P * h : P * (h + 1)], rep[:, h, :], ident_f[:])
+                    nc.scalar.copy(out=rz_all[:], in_=rzb[:])
 
         def evacuate(b, src):
             nc.vector.tensor_copy(out=xe[b][:], in_=src[:].rearrange("p (q t) -> p t q", t=4))

@@ -25,7 +25,7 @@ EPS = 1e-6
 A_BANKS = 5
 A_COLS = A_BANKS * 512
 RING = 9
-B_GROUPS = ((0, 4), (4, 4), (8, 4), (12, 2), (14, 1), (15, 1))
+B_LOADS = ((0, 4, 0, 4), (4, 4, 0, 4), (8, 4, 0, 4), (12, 2, 0, 4), (14, 2, 0, 2), (14, 2, 2, 2))
 
 FLOPS = 2 * P * F_DIM * E_DIM + 2 * HEADS * P * P * E_DIM
 
@@ -53,9 +53,13 @@ def tile_affnet_w_kernel(tc, X, W_words, W_scales, Z, beta, out):
         xeplane = keep.tile([P, G2 * P], U8, name="xeplane", tag="xeplane", align_bytes=64)
         ident_f = keep.tile([P, P], F32, name="ident_f", tag="ident_f")
         ident_b = keep.tile([P, P], BF16, name="ident_b", tag="ident_b")
-        beta_b = keep.tile([P, 1], BF16, name="beta_b", tag="beta_b")
+        beta_row = keep.tile([P, 2], BF16, name="beta_row", tag="beta_row")
+        ones_b = keep.tile([P, P], BF16, name="ones_b", tag="ones_b")
         beta_f = keep.tile([P, 1], F32, name="beta_f", tag="beta_f")
         half = keep.tile([P, 1], F32, name="half", tag="half")
+        ones = keep.tile([P, 1], F32, name="ones", tag="ones")
+        xet = keep.tile([P, 4, P], BF16, name="xet", tag="xet")
+        xsq = keep.tile([P, 4, P], F32, name="xsq", tag="xsq")
         zjunk = keep.tile([P, E_DIM], BF16, name="zjunk", tag="zjunk")
         xjunk = keep.tile([P, 512], BF16, name="xjunk", tag="xjunk")
         zss = keep.tile([P, HEADS], F32, name="zss", tag="zss")
@@ -80,10 +84,13 @@ def tile_affnet_w_kernel(tc, X, W_words, W_scales, Z, beta, out):
 
         for i in range(2):
             nc.sync.dma_start(out=x_sb[i][:], in_=X[:, 4096 * i : 4096 * (i + 1)])
-        nc.scalar.dma_start(out=beta_b[:], in_=beta.partition_broadcast(P))
+        nc.vector.memset(beta_row[:], 0.0)
+        nc.vector.memset(ones_b[:], 1.0)
+        nc.scalar.dma_start(out=beta_row[0:1, 0:1], in_=beta.rearrange("(a b) -> a b", a=1))
         for s in range(4):
             nc.vector.memset(planes[:, s, :].bitcast(I32), 0)
         nc.vector.memset(half[:], 0.5)
+        nc.vector.memset(ones[:], 1.0)
         make_identity(nc, ident_f[:])
         for s in range(4):
             for q in range(4):
@@ -96,30 +103,25 @@ def tile_affnet_w_kernel(tc, X, W_words, W_scales, Z, beta, out):
         for h in range(HEADS):
             nc.sync.dma_start(out=z_sb[h][:], in_=Z[h])
 
-        w_loads = [("A", g, 1) for g in range(G1)] + [("B", g0, n) for (g0, n) in B_GROUPS]
+        w_loads = [(g, 1, 0, A_COLS) for g in range(G1)]
+        w_loads += [(g0, n, A_COLS + P * t0, P * nt) for (g0, n, t0, nt) in B_LOADS]
         w_tiles = {}
 
         def load_w(i):
             if i >= len(w_loads):
                 return
-            kind, g0, n = w_loads[i]
-            if kind == "A":
-                wt = ring.tile([P, A_COLS], I32, name="wa%d" % g0, tag="w", align_bytes=64)
-                src = W_words[g0].rearrange("p n t -> p (n t)")[:, 0 : 4 * A_COLS].bitcast(I32)
-            else:
-                wt = ring.tile([P, n, 512], I32, name="wb%d" % g0, tag="w", align_bytes=64)
-                src = (
-                    W_words[g0 : g0 + n]
-                    .rearrange("g p n t -> p g (n t)")[:, :, 4 * A_COLS : 4 * E_DIM]
-                    .bitcast(I32)
-                )
+            g0, n, c0, width = w_loads[i]
+            wt = ring.tile([P, n, width], I32, name="w%d" % i, tag="w", align_bytes=64)
+            src = (
+                W_words[g0 : g0 + n]
+                .rearrange("g p n t -> p g (n t)")[:, :, 4 * c0 : 4 * (c0 + width)]
+                .bitcast(I32)
+            )
             nc.sync.dma_start(out=wt[:], in_=src)
             w_tiles[i] = wt
 
         for i in range(RING):
             load_w(i)
-
-        nc.vector.tensor_copy(out=beta_f[:], in_=beta_b[:])
 
         def flip_words(words_of, dst, part, bank_i, label, engine):
             bk = bank(bank_i, label)
@@ -173,13 +175,34 @@ def tile_affnet_w_kernel(tc, X, W_words, W_scales, Z, beta, out):
             )
 
         with tc.manual_schedule(engines={ENG.PE, ENG.DVE, ENG.Activation}):
+            def flip_last(dst, part, bank_i, label, engine):
+                bk = bank(bank_i, label, (P, 2, 4, P), BF16)
+                for a in range(2):
+                    for t in range(4):
+                        lo = E_DIM - 512 + P * t
+                        nc.tensor.transpose(
+                            bk[:, a, t, :], z_sb[2 * part + a][:, lo : lo + P], ident_b[:]
+                        )
+                o = dst[:, 1024 * part : 1024 * (part + 1)].rearrange(
+                    "p (a n t) -> p a n t", a=2, t=4
+                )
+                i = bk[:].rearrange("p a t n -> p a n t")
+                if engine == "v":
+                    nc.vector.tensor_copy(out=o, in_=i)
+                else:
+                    nc.scalar.copy(out=o, in_=i)
+
             jobs = [(x_words, j, xcodes, xplane) for j in range(4)]
             jobs += [(z_words, c, zcodes, zplane) for c in range(G2)]
             pending = None
             for i, (words, j, codes, plane) in enumerate(jobs):
                 og = grp.tile([P, 2048], BF16, name="og%d" % i, tag="grp", align_bytes=64)
-                flip_words(words(j, 0), og, 0, (2 * i) % 8, "ot%da" % i, "v")
-                flip_words(words(j, 1), og, 1, (2 * i + 1) % 8, "ot%db" % i, "s")
+                if i < len(jobs) - 1:
+                    flip_words(words(j, 0), og, 0, (2 * i) % 8, "ot%da" % i, "v")
+                    flip_words(words(j, 1), og, 1, (2 * i + 1) % 8, "ot%db" % i, "s")
+                else:
+                    flip_last(og, 0, (2 * i) % 8, "ot%da" % i, "v")
+                    flip_last(og, 1, (2 * i + 1) % 8, "ot%db" % i, "s")
                 if pending is not None:
                     quant(*pending)
                 pending = (og[:], codes, plane, 512 * j, 512)
@@ -189,7 +212,7 @@ def tile_affnet_w_kernel(tc, X, W_words, W_scales, Z, beta, out):
             for g in range(G1):
                 wt = w_tiles[g]
                 for b in range(A_BANKS):
-                    w_pass(acc[b], g, wt[:, 512 * b : 512 * (b + 1)], 512 * b)
+                    w_pass(acc[b], g, wt[:, 0, 512 * b : 512 * (b + 1)], 512 * b)
                 load_w(g + RING)
                 if g < HEADS:
                     nc.scalar.activation(
@@ -203,6 +226,11 @@ def tile_affnet_w_kernel(tc, X, W_words, W_scales, Z, beta, out):
                         out=rep[:], in_=rz[:].unsqueeze(2).to_broadcast([P, HEADS, P])
                     )
                 if g == 10:
+                    beta_all = bank(6, "beta_all", (P, 1))
+                    nc.tensor.matmul(
+                        out=beta_all[:], lhsT=ones_b[:], rhs=beta_row[:, 0:1], start=True, stop=True
+                    )
+                    nc.vector.tensor_copy(out=beta_f[:], in_=beta_all[:])
                     rzb = bank(7, "rzb")
                     for h in range(HEADS):
                         nc.tensor.transpose(rzb[:, P * h : P * (h + 1)], rep[:, h, :], ident_f[:])
@@ -229,8 +257,6 @@ def tile_affnet_w_kernel(tc, X, W_words, W_scales, Z, beta, out):
                 nc.scalar.copy(out=o, in_=src)
             quant(xeg[:], xecodes, xeplane, P * bs[0], P * n)
 
-        aff = bank(6, "aff")
-
         def aff_pass(c):
             nc.tensor.matmul_mx(
                 out=aff[:],
@@ -242,38 +268,65 @@ def tile_affnet_w_kernel(tc, X, W_words, W_scales, Z, beta, out):
                 stop=(c == G2 - 1),
             )
 
-        acc_b = bank(5, "accb")
-
-        def b_passes(i):
-            kind, g0, n = w_loads[i]
-            wt = w_tiles[i]
-            for gi in range(n):
-                w_pass(acc_b, g0 + gi, wt[:, gi, :], A_COLS)
-            load_w(i + RING)
-
         for b in range(A_BANKS):
             evacuate(b, acc[b])
         nc.vector.tensor_reduce(out=xss_a[:], in_=xss[:, 0:A_BANKS], op=ALU.add, axis=AX.X)
-        flip_xe([0, 1], 7, "s")
+
+        acc_t = [bank(b, "acct%d" % b, (P, P)) for b in (5, 6, 7, 0)]
+
+        def b_passes(i):
+            g0, n, c0, width = w_loads[i]
+            wt = w_tiles[i]
+            for gi in range(n):
+                g = g0 + gi
+                k = 4 * (g % 4)
+                for col in range(c0, c0 + width, P):
+                    t = (col - A_COLS) // P
+                    nc.tensor.matmul_mx(
+                        out=acc_t[t][:],
+                        lhsT=wt[:, gi, col - c0 : col - c0 + P].bitcast(FP8X4),
+                        lhsT_scale=planes[k:P, g // 4, col : col + P],
+                        rhs=xcodes[:, P * g : P * (g + 1)].bitcast(FP8X4),
+                        rhs_scale=xplane[:, P * g : P * (g + 1)],
+                        start=(g == 0),
+                        stop=(g == G1 - 1),
+                    )
+            load_w(i + RING)
+
+        ctx.enter_context(tc.manual_schedule(engines={ENG.PE}))
         b_passes(G1)
-        flip_xe([2, 3], 0, "s")
-        flip_xe([4], 1, "s")
-        aff_pass(0)
-        aff_pass(1)
+        flip_xe([0, 1], 1, "s")
         b_passes(G1 + 1)
-        aff_pass(2)
-        aff_pass(3)
-        aff_pass(4)
+        flip_xe([2, 3], 2, "s")
+        flip_xe([4], 3, "v")
+        aff = bank(4, "aff")
         for i in range(G1 + 2, len(w_loads)):
             b_passes(i)
 
         last = G2 - 1
-        evacuate(last, acc_b)
-        nc.scalar.activation(
-            out=xn[:], in_=xss[:, last : last + 1], func=ACT.Sqrt, bias=xss_a[:, 0:1]
+        for t in range(4):
+            nc.vector.tensor_copy(out=xet[:, t, :], in_=acc_t[t][:])
+            u = t ^ 1
+            nc.scalar.activation(out=xsq[:, u, :], in_=acc_t[u][:], func=ACT.Square)
+        xeg = xegp.tile([P, 512], BF16, name="xeg5", tag="xeg", align_bytes=64)
+        nc.vector.tensor_copy(
+            out=xeg[:].rearrange("p (m t) -> p m t", t=4), in_=xet[:].rearrange("p t m -> p m t")
         )
+        quant(xeg[:], xecodes, xeplane, P * last, P)
+        sums = bank(2, "sums", (P, 1))
+        aff_pass(0)
+        aff_pass(1)
+        for t in range(4):
+            u = t ^ 1
+            nc.tensor.matmul(
+                out=sums[:], lhsT=xsq[:, u, :], rhs=ones[:], start=(t == 0), stop=(t == 3)
+            )
+            if t == 1:
+                aff_pass(2)
+        aff_pass(3)
+        aff_pass(4)
+        nc.scalar.activation(out=xn[:], in_=sums[:], func=ACT.Sqrt, bias=xss_a[:, 0:1])
         nc.scalar.activation(out=lnjunk[:], in_=xn[:], func=ACT.Ln)
-        flip_xe([last], 2, "v")
         nc.vector.tensor_scalar_add(out=xne[:], in0=xn[:], scalar1=EPS)
         nc.vector.reciprocal(out=rx[:], in_=xne[:])
         aff_pass(last)

from contextlib import ExitStack

import concourse.mybir as mybir
from concourse.masks import make_identity

BF16 = mybir.dt.bfloat16
F32 = mybir.dt.float32
I32 = mybir.dt.int32
U32 = mybir.dt.uint32
U8 = mybir.dt.uint8
FP8X4 = mybir.dt.float8_e4m3fn_x4
ACT = mybir.ActivationFunctionType
ALU = mybir.AluOpType
ENG = mybir.EngineType
AX = mybir.AxisListType

P = 128
F_DIM = 8192
E_DIM = 3072
HEADS = 4
K_PASS = 512
G1 = F_DIM // K_PASS
G2 = E_DIM // K_PASS
EPS = 1e-6
A_BANKS = 5
A_COLS = A_BANKS * 512
RING = 9
B_LOADS = ((0, 4, 0, 4), (4, 4, 0, 4), (8, 4, 0, 4), (12, 2, 0, 4), (14, 2, 0, 2), (14, 2, 2, 2))

FLOPS = 2 * P * F_DIM * E_DIM + 2 * HEADS * P * P * E_DIM


def tile_affnet_w_kernel(tc, X, W_words, W_scales, Z, beta, out):
    nc = tc.nc
    with ExitStack() as ctx:
        keep = ctx.enter_context(tc.tile_pool(name="keep", bufs=1))
        grp = ctx.enter_context(tc.tile_pool(name="grp", bufs=3))
        ring = ctx.enter_context(tc.tile_pool(name="ring", bufs=RING))
        xegp = ctx.enter_context(tc.tile_pool(name="xegp", bufs=2))
        psum = ctx.enter_context(tc.psum_pool(name="psum", bufs=1))

        def bank(i, label, shape=(P, 512), dtype=F32):
            return psum.tile(list(shape), dtype, tag="bank%d" % i, name=label)

        x_sb = [keep.tile([P, 4096], BF16, name="x%d" % i, tag="x%d" % i) for i in range(2)]
        z_sb = [keep.tile([P, E_DIM], BF16, name="z%d" % h, tag="z%d" % h) for h in range(HEADS)]
        planes = keep.tile([P, 4, E_DIM], U8, name="planes", tag="planes", align_bytes=64)
        xcodes = keep.tile([P, G1 * P], U32, name="xcodes", tag="xcodes", align_bytes=64)
        xplane = keep.tile([P, G1 * P], U8, name="xplane", tag="xplane", align_bytes=64)
        zcodes = keep.tile([P, G2 * 512], U32, name="zcodes", tag="zcodes", align_bytes=64)
        zplane = keep.tile([P, G2 * 512], U8, name="zplane", tag="zplane", align_bytes=64)
        xecodes = keep.tile([P, G2 * P], U32, name="xecodes", tag="xecodes", align_bytes=64)
        xeplane = keep.tile([P, G2 * P], U8, name="xeplane", tag="xeplane", align_bytes=64)
        ident_f = keep.tile([P, P], F32, name="ident_f", tag="ident_f")
        ident_b = keep.tile([P, P], BF16, name="ident_b", tag="ident_b")
        beta_row = keep.tile([P, 2], BF16, name="beta_row", tag="beta_row")
        ones_b = keep.tile([P, P], BF16, name="ones_b", tag="ones_b")
        beta_f = keep.tile([P, 1], F32, name="beta_f", tag="beta_f")
        half = keep.tile([P, 1], F32, name="half", tag="half")
        ones = keep.tile([P, 1], F32, name="ones", tag="ones")
        xet = keep.tile([P, 4, P], BF16, name="xet", tag="xet")
        xsq = keep.tile([P, 4, P], F32, name="xsq", tag="xsq")
        zjunk = keep.tile([P, E_DIM], BF16, name="zjunk", tag="zjunk")
        xjunk = keep.tile([P, 512], BF16, name="xjunk", tag="xjunk")
        zss = keep.tile([P, HEADS], F32, name="zss", tag="zss")
        zn = keep.tile([P, HEADS], F32, name="zn", tag="zn")
        zne = keep.tile([P, HEADS], F32, name="zne", tag="zne")
        rz = keep.tile([P, HEADS], F32, name="rz", tag="rz")
        rep = keep.tile([P, HEADS, P], F32, name="rep", tag="rep")
        rz_all = keep.tile([P, HEADS * P], F32, name="rz_all", tag="rz_all")
        xss = keep.tile([P, G2], F32, name="xss", tag="xss")
        xss_a = keep.tile([P, 1], F32, name="xss_a", tag="xss_a")
        xn = keep.tile([P, 1], F32, name="xn", tag="xn")
        lnjunk = keep.tile([P, 1], F32, name="lnjunk", tag="lnjunk")
        xne = keep.tile([P, 1], F32, name="xne", tag="xne")
        rx = keep.tile([P, 1], F32, name="rx", tag="rx")
        scaled = keep.tile([P, HEADS * P], F32, name="scaled", tag="scaled")
        max2 = keep.tile([P, 2 * P], F32, name="max2", tag="max2")
        cosT = keep.tile([P, P], F32, name="cosT", tag="cosT")
        sym = keep.tile([P, P], F32, name="sym", tag="sym")
        logv = keep.tile([P, P], F32, name="logv", tag="logv")
        res = keep.tile([P, P], F32, name="res", tag="res")
        xe = [keep.tile([P, 4, P], BF16, name="xe%d" % b, tag="xe%d" % b) for b in range(G2)]

        for i in range(2):
            nc.sync.dma_start(out=x_sb[i][:], in_=X[:, 4096 * i : 4096 * (i + 1)])
        nc.vector.memset(beta_row[:], 0.0)
        nc.vector.memset(ones_b[:], 1.0)
        nc.scalar.dma_start(out=beta_row[0:1, 0:1], in_=beta.rearrange("(a b) -> a b", a=1))
        for s in range(4):
            nc.vector.memset(planes[:, s, :].bitcast(I32), 0)
        nc.vector.memset(half[:], 0.5)
        nc.vector.memset(ones[:], 1.0)
        make_identity(nc, ident_f[:])
        for s in range(4):
            for q in range(4):
                nc.gpsimd.dma_start(
                    out=planes[32 * q : 32 * q + 16, s, :].bitcast(F32),
                    in_=W_scales[4 * s : 4 * s + 4, 4 * q : 4 * q + 4, :].bitcast(F32),
                )
            if s == 0:
                make_identity(nc, ident_b[:])
        for h in range(HEADS):
            nc.sync.dma_start(out=z_sb[h][:], in_=Z[h])

        w_loads = [(g, 1, 0, A_COLS) for g in range(G1)]
        w_loads += [(g0, n, A_COLS + P * t0, P * nt) for (g0, n, t0, nt) in B_LOADS]
        w_tiles = {}

        def load_w(i):
            if i >= len(w_loads):
                return
            g0, n, c0, width = w_loads[i]
            wt = ring.tile([P, n, width], I32, name="w%d" % i, tag="w", align_bytes=64)
            src = (
                W_words[g0 : g0 + n]
                .rearrange("g p n t -> p g (n t)")[:, :, 4 * c0 : 4 * (c0 + width)]
                .bitcast(I32)
            )
            nc.sync.dma_start(out=wt[:], in_=src)
            w_tiles[i] = wt

        for i in range(RING):
            load_w(i)

        def flip_words(words_of, dst, part, bank_i, label, engine):
            bk = bank(bank_i, label)
            for a in range(2):
                for u in range(2):
                    nc.tensor.transpose(
                        bk[:, (2 * a + u) * P : (2 * a + u + 1) * P], words_of(a, u), ident_f[:]
                    )
            o = dst[:].bitcast(F32)[:, 512 * part : 512 * (part + 1)].rearrange(
                "p (a n u) -> p a n u", a=2, u=2
            )
            i = bk[:].rearrange("p (a u n) -> p a n u", a=2, u=2)
            if engine == "v":
                nc.vector.tensor_copy(out=o, in_=i)
            else:
                nc.scalar.copy(out=o, in_=i)

        def quant(src, codes, plane, lo, width):
            nc.vector.quantize_mx(
                out=codes[:, lo : lo + width].bitcast(FP8X4),
                scales=plane[:, lo : lo + width],
                in_=src,
            )

        def x_words(j, part):
            def pick(a, u):
                g = 4 * j + 2 * part + a
                xw = x_sb[g // 8][:].bitcast(F32)
                lo = 256 * (g % 8)
                return xw[:, lo + u : lo + 256 : 2]

            return pick

        def z_words(c, part):
            def pick(a, u):
                zw = z_sb[2 * part + a][:].bitcast(F32)
                return zw[:, 256 * c + u : 256 * (c + 1) : 2]

            return pick

        def w_pass(acc, g, codes, col0):
            k = 4 * (g % 4)
            nc.tensor.matmul_mx(
                out=acc[:],
                lhsT=xcodes[:, P * g : P * (g + 1)].bitcast(FP8X4),
                lhsT_scale=xplane[:, P * g : P * (g + 1)],
                rhs=codes.bitcast(FP8X4),
                rhs_scale=planes[k:P, g // 4, col0 : col0 + 512],
                start=(g == 0),
                stop=(g == G1 - 1),
            )

        with tc.manual_schedule(engines={ENG.PE, ENG.DVE, ENG.Activation}):
            def flip_last(dst, part, bank_i, label, engine):
                bk = bank(bank_i, label, (P, 2, 4, P), BF16)
                for a in range(2):
                    for t in range(4):
                        lo = E_DIM - 512 + P * t
                        nc.tensor.transpose(
                            bk[:, a, t, :], z_sb[2 * part + a][:, lo : lo + P], ident_b[:]
                        )
                o = dst[:, 1024 * part : 1024 * (part + 1)].rearrange(
                    "p (a n t) -> p a n t", a=2, t=4
                )
                i = bk[:].rearrange("p a t n -> p a n t")
                if engine == "v":
                    nc.vector.tensor_copy(out=o, in_=i)
                else:
                    nc.scalar.copy(out=o, in_=i)

            jobs = [(x_words, j, xcodes, xplane) for j in range(4)]
            jobs += [(z_words, c, zcodes, zplane) for c in range(G2)]
            pending = None
            for i, (words, j, codes, plane) in enumerate(jobs):
                og = grp.tile([P, 2048], BF16, name="og%d" % i, tag="grp", align_bytes=64)
                if i < len(jobs) - 1:
                    flip_words(words(j, 0), og, 0, (2 * i) % 8, "ot%da" % i, "v")
                    flip_words(words(j, 1), og, 1, (2 * i + 1) % 8, "ot%db" % i, "s")
                else:
                    flip_last(og, 0, (2 * i) % 8, "ot%da" % i, "v")
                    flip_last(og, 1, (2 * i + 1) % 8, "ot%db" % i, "s")
                if pending is not None:
                    quant(*pending)
                pending = (og[:], codes, plane, 512 * j, 512)
            quant(*pending)

            acc = [bank(b, "acc%d" % b) for b in range(A_BANKS)]
            for g in range(G1):
                wt = w_tiles[g]
                for b in range(A_BANKS):
                    w_pass(acc[b], g, wt[:, 0, 512 * b : 512 * (b + 1)], 512 * b)
                load_w(g + RING)
                if g < HEADS:
                    nc.scalar.activation(
                        out=zjunk[:], in_=z_sb[g][:], func=ACT.Square, accum_out=zss[:, g : g + 1]
                    )
                if g == HEADS:
                    nc.scalar.activation(out=zn[:], in_=zss[:], func=ACT.Sqrt)
                    nc.vector.tensor_scalar_add(out=zne[:], in0=zn[:], scalar1=EPS)
                    nc.vector.reciprocal(out=rz[:], in_=zne[:])
                    nc.vector.tensor_copy(
                        out=rep[:], in_=rz[:].unsqueeze(2).to_broadcast([P, HEADS, P])
                    )
                if g == 10:
                    beta_all = bank(6, "beta_all", (P, 1))
                    nc.tensor.matmul(
                        out=beta_all[:], lhsT=ones_b[:], rhs=beta_row[:, 0:1], start=True, stop=True
                    )
                    nc.vector.tensor_copy(out=beta_f[:], in_=beta_all[:])
                    rzb = bank(7, "rzb")
                    for h in range(HEADS):
                        nc.tensor.transpose(rzb[:, P * h : P * (h + 1)], rep[:, h, :], ident_f[:])
                    nc.scalar.copy(out=rz_all[:], in_=rzb[:])

        def evacuate(b, src):
            nc.vector.tensor_copy(out=xe[b][:], in_=src[:].rearrange("p (q t) -> p t q", t=4))
            nc.scalar.activation(
                out=xjunk[:], in_=src[:], func=ACT.Square, accum_out=xss[:, b : b + 1]
            )

        def flip_xe(bs, bank_i, engine):
            n = len(bs)
            xt = bank(bank_i, "xet%d" % bs[0], (P, n, 4, P), BF16)
            for i, b in enumerate(bs):
                for t in range(4):
                    nc.tensor.transpose(xt[:, i, t, :], xe[b][:, t, :], ident_b[:])
            xeg = xegp.tile([P, n * 512], BF16, name="xeg%d" % bs[0], tag="xeg", align_bytes=64)
            o = xeg[:].rearrange("p (i n t) -> p i n t", i=n, t=4)
            src = xt[:].rearrange("p i t n -> p i n t")
            if engine == "v":
                nc.vector.tensor_copy(out=o, in_=src)
            else:
                nc.scalar.copy(out=o, in_=src)
            quant(xeg[:], xecodes, xeplane, P * bs[0], P * n)

        def aff_pass(c):
            nc.tensor.matmul_mx(
                out=aff[:],
                lhsT=xecodes[:, P * c : P * (c + 1)].bitcast(FP8X4),
                lhsT_scale=xeplane[:, P * c : P * (c + 1)],
                rhs=zcodes[:, 512 * c : 512 * (c + 1)].bitcast(FP8X4),
                rhs_scale=zplane[:, 512 * c : 512 * (c + 1)],
                start=(c == 0),
                stop=(c == G2 - 1),
            )

        for b in range(A_BANKS):
            evacuate(b, acc[b])
        nc.vector.tensor_reduce(out=xss_a[:], in_=xss[:, 0:A_BANKS], op=ALU.add, axis=AX.X)

        acc_t = [bank(b, "acct%d" % b, (P, P)) for b in (5, 6, 7, 0)]

        def b_passes(i):
            g0, n, c0, width = w_loads[i]
            wt = w_tiles[i]
            for gi in range(n):
                g = g0 + gi
                k = 4 * (g % 4)
                for col in range(c0, c0 + width, P):
                    t = (col - A_COLS) // P
                    nc.tensor.matmul_mx(
                        out=acc_t[t][:],
                        lhsT=wt[:, gi, col - c0 : col - c0 + P].bitcast(FP8X4),
                        lhsT_scale=planes[k:P, g // 4, col : col + P],
                        rhs=xcodes[:, P * g : P * (g + 1)].bitcast(FP8X4),
                        rhs_scale=xplane[:, P * g : P * (g + 1)],
                        start=(g == 0),
                        stop=(g == G1 - 1),
                    )
            load_w(i + RING)

        ctx.enter_context(tc.manual_schedule(engines={ENG.PE}))
        b_passes(G1)
        flip_xe([0, 1], 1, "s")
        b_passes(G1 + 1)
        flip_xe([2, 3], 2, "s")
        flip_xe([4], 3, "v")
        aff = bank(4, "aff")
        for i in range(G1 + 2, len(w_loads)):
            b_passes(i)

        last = G2 - 1
        for t in range(4):
            nc.vector.tensor_copy(out=xet[:, t, :], in_=acc_t[t][:])
            u = t ^ 1
            nc.scalar.activation(out=xsq[:, u, :], in_=acc_t[u][:], func=ACT.Square)
        xeg = xegp.tile([P, 512], BF16, name="xeg5", tag="xeg", align_bytes=64)
        nc.vector.tensor_copy(
            out=xeg[:].rearrange("p (m t) -> p m t", t=4), in_=xet[:].rearrange("p t m -> p m t")
        )
        quant(xeg[:], xecodes, xeplane, P * last, P)
        sums = bank(2, "sums", (P, 1))
        aff_pass(0)
        aff_pass(1)
        for t in range(4):
            u = t ^ 1
            nc.tensor.matmul(
                out=sums[:], lhsT=xsq[:, u, :], rhs=ones[:], start=(t == 0), stop=(t == 3)
            )
            if t == 1:
                aff_pass(2)
        aff_pass(3)
        aff_pass(4)
        nc.scalar.activation(out=xn[:], in_=sums[:], func=ACT.Sqrt, bias=xss_a[:, 0:1])
        nc.scalar.activation(out=lnjunk[:], in_=xn[:], func=ACT.Ln)
        nc.vector.tensor_scalar_add(out=xne[:], in0=xn[:], scalar1=EPS)
        nc.vector.reciprocal(out=rx[:], in_=xne[:])
        aff_pass(last)

        nc.vector.scalar_tensor_tensor(
            out=scaled[:], in0=aff[:], scalar=rx[:, 0:1], in1=rz_all[:], op0=ALU.mult, op1=ALU.mult
        )
        nc.vector.tensor_max(out=max2[:], in0=scaled[:, 0 : 2 * P], in1=scaled[:, 2 * P : 4 * P])
        nc.vector.tensor_max(out=cosT[:], in0=max2[:, 0:P], in1=max2[:, P : 2 * P])
        cos_b = bank(3, "cosb")
        nc.tensor.transpose(cos_b[:, 0:P], cosT[:], ident_f[:])
        nc.vector.tensor_add(out=sym[:], in0=cosT[:], in1=cos_b[:, 0:P])
        nc.scalar.activation(out=logv[:], in_=sym[:], func=ACT.Ln, scale=0.25, bias=half[:, 0:1])
        nc.scalar.activation(out=res[:], in_=logv[:], func=ACT.Exp, scale=beta_f[:, 0:1])
        nc.sync.dma_start(out=out[:, :], in_=res[:])
